import numpy as np
import ml_dtypes


def mxq(x, axis, fmt="e4m3"):
    dtype, down = {"e4m3": (ml_dtypes.float8_e4m3fn, 7), "e5m2": (ml_dtypes.float8_e5m2, 14)}[fmt]
    v = np.moveaxis(np.asarray(x, np.float32).astype(ml_dtypes.bfloat16).astype(np.float64), axis, -1)
    blocks = v.reshape(v.shape[:-1] + (-1, 32))
    amax = np.abs(blocks).max(-1, keepdims=True)
    byte = np.maximum(np.where(amax > 0, np.frexp(amax)[1] - 1 + 127, 0) - down, 1)
    scale = np.exp2(byte - 127.0)
    codes = (blocks / scale).astype(np.float32).astype(dtype).astype(np.float64)
    return np.moveaxis((codes * scale).reshape(v.shape), -1, axis)


WIDE = False


def mx_kscale(k):
    if not WIDE:
        return np.ones(k)
    levels = np.array([10, -10, 5, -5, 0])
    a = np.random.permutation(np.resize(levels, k // 512 * 4)).reshape(k // 512, 4)
    idx = np.arange(k)
    return np.exp2(a[idx // 512, idx % 128 // 32])


BF16 = ml_dtypes.bfloat16


def bf(x):
    return np.asarray(x, np.float32).astype(BF16)


def f64(x):
    return np.asarray(x).astype(np.float64)


E2M1 = np.array([0.0, 0.5, 1.0, 1.5, 2.0, 3.0, 4.0, 6.0, -0.0, -0.5, -1.0, -1.5, -2.0, -3.0, -4.0, -6.0])


def pack_weight(w, fmt):
    k, n = w.shape
    w = f64(bf(w)).reshape(k // 32, 32, n)
    amax = np.abs(w).max(1)
    if fmt == "e4m3":
        byte = np.frexp(amax)[1] - 1 + 127 - 7
    else:
        mant, ex = np.frexp(amax / 6.0)
        byte = np.where(mant > 0.5, ex, ex - 1) + 127
    byte = np.clip(np.where(amax > 0, byte, 1), 1, 254)
    scaled = (w * np.exp2(127.0 - byte)[:, None, :]).reshape(k, n).astype(np.float32)
    by_word = np.ascontiguousarray(scaled.reshape(k // 512, 128, 4, n).transpose(0, 1, 3, 2))
    if fmt == "e4m3":
        words = by_word.astype(ml_dtypes.float8_e4m3fn).view(np.uint8)
    else:
        c = by_word.astype(ml_dtypes.float4_e2m1fn).view(np.uint8) & 0xF
        words = c[..., 0::2] | (c[..., 1::2] << 4)
    return np.ascontiguousarray(words), np.ascontiguousarray(byte.astype(np.uint8).reshape(k // 512, 16, n))


def unpack_weight(words, scales, fmt):
    g, p, n, _ = words.shape
    if fmt == "e4m3":
        vals = np.ascontiguousarray(words).view(ml_dtypes.float8_e4m3fn).astype(np.float64)
    else:
        nib = np.empty((g, p, n, 4), np.uint8)
        nib[..., 0::2] = words & 0xF
        nib[..., 1::2] = words >> 4
        vals = E2M1[nib]
    vals = vals * np.repeat(np.exp2(scales.astype(np.float64) - 127.0), 8, axis=1)[..., None]
    return vals.transpose(0, 1, 3, 2).reshape(g * 512, n)


T, S, B, E, Z = 512, 512, 2, 1024, 128


def sigmoid(v):
    return 1.0 / (1.0 + np.exp(-v))


def setup_inputs():
    t = mx_kscale(E)
    query = bf(np.random.standard_normal((T, B, E)))
    hr = bf(np.random.standard_normal((T, B, E)) * 0.2 * t)
    Wu = np.random.standard_normal((E, E)) / np.sqrt(E)
    bu = bf(np.random.standard_normal(E) * 0.3)
    Wh = np.random.standard_normal((E, E)) * 5.0 / np.sqrt(E) / t[None, :]
    bh = bf(np.random.standard_normal(E) * 0.3)
    Wu_words, Wu_scales = pack_weight(np.ascontiguousarray(Wu.T), "e4m3")
    Wh_words, Wh_scales = pack_weight(np.ascontiguousarray(Wh.T), "e4m3")
    return {"query": query,
            "hr": hr,
            "Wu_words": Wu_words,
            "Wu_scales": Wu_scales,
            "bu": bu,
            "Wh_words": Wh_words,
            "Wh_scales": Wh_scales,
            "bh": bh}


def reference(query, hr, Wu_words, Wu_scales, bu, Wh_words, Wh_scales, bh):
    x = f64(query)
    u = sigmoid((mxq(x, 2, "e4m3") @ unpack_weight(Wu_words, Wu_scales, "e4m3")) + f64(bu))
    h = np.tanh((mxq(f64(hr), 2, "e4m3") @ unpack_weight(Wh_words, Wh_scales, "e4m3")) + f64(bh))
    return x + u * (h - x)

@@ -1,0 +1,242 @@
+from contextlib import ExitStack
+
+import concourse.mybir as mybir
+from concourse.masks import make_identity
+
+F32 = mybir.dt.float32
+BF16 = mybir.dt.bfloat16
+I32 = mybir.dt.int32
+U32 = mybir.dt.uint32
+U8 = mybir.dt.uint8
+FP8X4 = mybir.dt.float8_e4m3fn_x4
+ACT = mybir.ActivationFunctionType
+ALU = mybir.AluOpType
+
+P = 128
+TOKENS = 1024
+FEATURES = 1024
+K_PASS = 4 * P
+K_GROUPS = FEATURES // K_PASS
+WORDS = K_PASS // 2
+SLOTS = TOKENS // P
+QUARTER_SLOTS = 2
+QUARTERS = SLOTS // QUARTER_SLOTS
+QUARTER_TOKENS = QUARTER_SLOTS * P
+BLOCKS = FEATURES // P
+STEP_BLOCKS = 2
+STEP_FEATURES = STEP_BLOCKS * P
+QUARTER_STEPS = BLOCKS // STEP_BLOCKS
+STEPS = QUARTERS * QUARTER_STEPS
+
+GATE, CANDIDATE = 0, 1
+PATHS = (GATE, CANDIDATE)
+PATH_NAMES = ("gate", "candidate")
+FUNCTIONS = (ACT.Sigmoid, ACT.Tanh)
+
+FLOPS = 2 * 2 * TOKENS * FEATURES * FEATURES
+
+
+def tile_gatedcrossattention_pb_kernel(
+    tc, query, hr, Wu_words, Wu_scales, bu, Wh_words, Wh_scales, bh, out
+):
+    nc = tc.nc
+
+    rows_dram = [
+        x.flatten_outer_dims().rearrange("(p s) e -> p s e", s=SLOTS) for x in (query, hr)
+    ]
+    out_dram = out.flatten_outer_dims().rearrange("(p s) e -> p s e", s=SLOTS)
+    w_codes_dram = [
+        w.rearrange("g p n t -> p g (n t)").bitcast(I32) for w in (Wu_words, Wh_words)
+    ]
+    w_scales_dram = [Wu_scales, Wh_scales]
+    bias_dram = [b.rearrange("(b n) -> b n", n=P) for b in (bu, bh)]
+
+    with ExitStack() as ctx:
+        keep = ctx.enter_context(tc.tile_pool(name="keep", bufs=1))
+        stage = ctx.enter_context(tc.tile_pool(name="stage", bufs=4))
+        turned = ctx.enter_context(tc.tile_pool(name="turned", bufs=3))
+        blend = ctx.enter_context(tc.tile_pool(name="blend", bufs=2))
+        results = ctx.enter_context(tc.tile_pool(name="results", bufs=4))
+        psum_in = ctx.enter_context(tc.psum_pool(name="psum_in", bufs=2))
+        psum_mx = ctx.enter_context(tc.psum_pool(name="psum_mx", bufs=2))
+        psum_back = ctx.enter_context(tc.psum_pool(name="psum_back", bufs=1))
+        ctx.enter_context(tc.manual_schedule())
+
+        rows = [
+            keep.tile([P, SLOTS, FEATURES], BF16, name="rows_" + PATH_NAMES[path])
+            for path in PATHS
+        ]
+        w_codes = [
+            keep.tile([P, K_GROUPS, FEATURES], U32, align_bytes=64, name="w_codes_" + PATH_NAMES[path])
+            for path in PATHS
+        ]
+        w_planes = keep.tile([P, FEATURES], U8, align_bytes=64)
+        x_codes = keep.tile([P, 2, QUARTERS, K_GROUPS, QUARTER_TOKENS], U32, align_bytes=64)
+        x_planes = keep.tile([P, 2, QUARTERS, K_GROUPS, QUARTER_TOKENS], U8, align_bytes=64)
+        identity = keep.tile([P, P], F32)
+        bias_rows = keep.tile([P, P], BF16)
+        bias_rows_f32 = keep.tile([P, P], F32)
+        bias_cols = keep.tile([P, 2 * BLOCKS], F32)
+        table_warmer = keep.tile([P, 1], F32)
+
+        def load_rows(quarter):
+            slots = slice(quarter * QUARTER_SLOTS, (quarter + 1) * QUARTER_SLOTS)
+            for path in PATHS:
+                nc.sync.dma_start(out=rows[path][:, slots, :], in_=rows_dram[path][:, slots, :])
+
+        def load_weight_scales():
+            for path in PATHS:
+                for quadrant in range(4):
+                    first = 32 * quadrant + 4 * K_GROUPS * path
+                    nc.sync.dma_start(
+                        out=w_planes[first : first + 4 * K_GROUPS, :].bitcast(I32),
+                        in_=w_scales_dram[path][:, 4 * quadrant : 4 * quadrant + 4, :].bitcast(I32),
+                    )
+
+        def load_weights(pair):
+            cols = slice(pair * STEP_FEATURES, (pair + 1) * STEP_FEATURES)
+            for path in PATHS:
+                nc.sync.dma_start(
+                    out=w_codes[path][:, :, cols].bitcast(I32), in_=w_codes_dram[path][:, :, cols]
+                )
+
+        def features_onto_partitions(path, quarter, group, copy):
+            flipped = psum_in.tile([P, 2, QUARTER_TOKENS], F32, name="flipped")
+            for h in range(2):
+                for j in range(QUARTER_SLOTS):
+                    words = rows[path][:, quarter * QUARTER_SLOTS + j, :].bitcast(F32)
+                    nc.tensor.transpose(
+                        flipped[:, h, j * P : (j + 1) * P],
+                        words[:, group * WORDS + h : (group + 1) * WORDS : 2],
+                        identity[:],
+                    )
+            grouped = stage.tile([P, 4 * QUARTER_TOKENS], BF16, align_bytes=64, name="grouped")
+            copy(
+                out=grouped[:].bitcast(F32).rearrange("p (c h) -> p c h", h=2),
+                in_=flipped[:].rearrange("p h c -> p c h"),
+            )
+            return (path, quarter, group, grouped)
+
+        def quantise(path, quarter, group, grouped):
+            nc.vector.quantize_mx(
+                out=x_codes[:, path, quarter, group, :].bitcast(FP8X4),
+                scales=x_planes[:, path, quarter, group, :],
+                in_=grouped[:],
+            )
+
+        def project(step):
+            quarter, pair = divmod(step, QUARTER_STEPS)
+            activated = []
+            for path in PATHS:
+                acc = psum_mx.tile([P, STEP_BLOCKS, QUARTER_TOKENS], F32, name="acc_" + PATH_NAMES[path])
+                for j in range(STEP_BLOCKS):
+                    block = pair * STEP_BLOCKS + j
+                    cols = slice(block * P, (block + 1) * P)
+                    for group in range(K_GROUPS):
+                        plane_start = 4 * (K_GROUPS * path + group)
+                        nc.tensor.matmul_mx(
+                            out=acc[:, j, :],
+                            lhsT=w_codes[path][:, group, cols].bitcast(FP8X4),
+                            lhsT_scale=w_planes[plane_start:P, cols],
+                            rhs=x_codes[:, path, quarter, group, :].bitcast(FP8X4),
+                            rhs_scale=x_planes[:, path, quarter, group, :],
+                            start=(group == 0),
+                            stop=(group == K_GROUPS - 1),
+                        )
+                value = turned.tile([P, STEP_BLOCKS, QUARTER_TOKENS], F32, name="turned_" + PATH_NAMES[path])
+                for j in range(STEP_BLOCKS):
+                    column = path * BLOCKS + pair * STEP_BLOCKS + j
+                    nc.scalar.activation(
+                        out=value[:, j, :],
+                        in_=acc[:, j, :],
+                        func=FUNCTIONS[path],
+                        bias=bias_cols[:, column : column + 1],
+                        scale=1.0,
+                    )
+                activated.append(value)
+            return activated
+
+        def tokens_onto_partitions(path, value):
+            back = psum_back.tile([P, QUARTER_SLOTS, STEP_FEATURES], F32, name="back_" + PATH_NAMES[path])
+            for s in range(QUARTER_SLOTS):
+                for j in range(STEP_BLOCKS):
+                    nc.tensor.transpose(
+                        back[:, s, j * P : (j + 1) * P], value[:, j, s * P : (s + 1) * P], identity[:]
+                    )
+            return back
+
+        def step_view(tensor, step):
+            quarter, pair = divmod(step, QUARTER_STEPS)
+            return tensor[
+                :,
+                quarter * QUARTER_SLOTS : (quarter + 1) * QUARTER_SLOTS,
+                pair * STEP_FEATURES : (pair + 1) * STEP_FEATURES,
+            ]
+
+        nc.vector.memset(w_planes[:].bitcast(I32), 0)
+        nc.vector.memset(bias_rows[:], 0.0)
+        nc.vector.memset(table_warmer[:], 0.0)
+        for path in PATHS:
+            nc.scalar.dma_start(
+                out=bias_rows[path * BLOCKS : (path + 1) * BLOCKS, :], in_=bias_dram[path]
+            )
+        nc.scalar.activation(out=table_warmer[:], in_=table_warmer[:], func=ACT.Sigmoid)
+        make_identity(nc, identity[:])
+
+        load_rows(0)
+        load_weight_scales()
+        load_weights(0)
+        load_weights(1)
+        load_rows(1)
+        load_weights(2)
+        load_weights(3)
+        load_rows(2)
+        load_rows(3)
+
+        nc.vector.tensor_copy(out=bias_rows_f32[:], in_=bias_rows[:])
+        for path in PATHS:
+            jobs = [
+                features_onto_partitions(path, 0, 0, nc.vector.tensor_copy),
+                features_onto_partitions(path, 0, 1, nc.scalar.copy),
+            ]
+            for job in jobs:
+                quantise(*job)
+        bias_flipped = psum_in.tile([P, 2, QUARTER_TOKENS], F32, name="flipped")
+        nc.tensor.transpose(bias_flipped[:, 0, 0:P], bias_rows_f32[:], identity[:])
+        nc.vector.tensor_copy(out=bias_cols[:], in_=bias_flipped[:, 0, 0 : 2 * BLOCKS])
+
+        activated = {}
+        difference = {}
+        product = {}
+        waiting = []
+        for r in range(STEPS + 2):
+            if r < STEPS:
+                activated[r] = project(r)
+            if 1 <= r <= STEPS:
+                u_t, c_t = activated[r - 1]
+                c_back = tokens_onto_partitions(CANDIDATE, c_t)
+                u_back = tokens_onto_partitions(GATE, u_t)
+                difference[r - 1] = blend.tile([P, QUARTER_SLOTS, STEP_FEATURES], F32, name="difference")
+                nc.vector.tensor_tensor(
+                    out=difference[r - 1][:], in0=c_back[:], in1=step_view(rows[GATE], r - 1), op=ALU.subtract
+                )
+            if r >= 2:
+                result = results.tile([P, QUARTER_SLOTS, STEP_FEATURES], F32, name="result")
+                nc.vector.tensor_tensor(
+                    out=result[:], in0=product[r - 2][:], in1=step_view(rows[GATE], r - 2), op=ALU.add
+                )
+                nc.sync.dma_start(out=step_view(out_dram, r - 2), in_=result[:])
+            if 1 <= r <= STEPS:
+                product[r - 1] = blend.tile([P, QUARTER_SLOTS, STEP_FEATURES], F32, name="product")
+                nc.vector.tensor_tensor(
+                    out=product[r - 1][:], in0=u_back[:], in1=difference[r - 1][:], op=ALU.mult
+                )
+            for job in waiting:
+                quantise(*job)
+            waiting = []
+            quarter, pair = divmod(r, QUARTER_STEPS)
+            if quarter + 1 < QUARTERS and pair in PATHS:
+                waiting = [
+                    features_onto_partitions(pair, quarter + 1, group, nc.scalar.copy)
+                    for group in range(K_GROUPS)
+                ]

@@ -58,8 +58,8 @@ def tile_gatedcrossattention_pb_kernel(
         blend = ctx.enter_context(tc.tile_pool(name="blend", bufs=2))
         results = ctx.enter_context(tc.tile_pool(name="results", bufs=4))
         psum_in = ctx.enter_context(tc.psum_pool(name="psum_in", bufs=2))
-        psum_mx = ctx.enter_context(tc.psum_pool(name="psum_mx", bufs=2))
-        psum_back = ctx.enter_context(tc.psum_pool(name="psum_back", bufs=1))
+        psum_mx = ctx.enter_context(tc.psum_pool(name="psum_mx", bufs=1))
+        psum_back = ctx.enter_context(tc.psum_pool(name="psum_back", bufs=2))
         ctx.enter_context(tc.manual_schedule())
 
         rows = [

@@ -206,31 +206,27 @@ def tile_gatedcrossattention_pb_kernel(
         nc.vector.tensor_copy(out=bias_cols[:], in_=bias_flipped[:, 0, 0 : 2 * BLOCKS])
 
         activated = {}
-        difference = {}
-        product = {}
         waiting = []
-        for r in range(STEPS + 2):
+        for r in range(STEPS + 1):
             if r < STEPS:
                 activated[r] = project(r)
             if 1 <= r <= STEPS:
                 u_t, c_t = activated[r - 1]
                 c_back = tokens_onto_partitions(CANDIDATE, c_t)
                 u_back = tokens_onto_partitions(GATE, u_t)
-                difference[r - 1] = blend.tile([P, QUARTER_SLOTS, STEP_FEATURES], F32, name="difference")
+                difference = blend.tile([P, QUARTER_SLOTS, STEP_FEATURES], F32, name="difference")
                 nc.vector.tensor_tensor(
-                    out=difference[r - 1][:], in0=c_back[:], in1=step_view(rows[GATE], r - 1), op=ALU.subtract
+                    out=difference[:], in0=c_back[:], in1=step_view(rows[GATE], r - 1), op=ALU.subtract
                 )
-            if r >= 2:
+                product = blend.tile([P, QUARTER_SLOTS, STEP_FEATURES], F32, name="product")
+                nc.vector.tensor_tensor(
+                    out=product[:], in0=u_back[:], in1=difference[:], op=ALU.mult
+                )
                 result = results.tile([P, QUARTER_SLOTS, STEP_FEATURES], F32, name="result")
-                nc.vector.tensor_tensor(
-                    out=result[:], in0=product[r - 2][:], in1=step_view(rows[GATE], r - 2), op=ALU.add
+                nc.gpsimd.tensor_tensor(
+                    out=result[:], in0=product[:], in1=step_view(rows[GATE], r - 1), op=ALU.add
                 )
-                nc.sync.dma_start(out=step_view(out_dram, r - 2), in_=result[:])
-            if 1 <= r <= STEPS:
-                product[r - 1] = blend.tile([P, QUARTER_SLOTS, STEP_FEATURES], F32, name="product")
-                nc.vector.tensor_tensor(
-                    out=product[r - 1][:], in0=u_back[:], in1=difference[r - 1][:], op=ALU.mult
-                )
+                nc.sync.dma_start(out=step_view(out_dram, r - 1), in_=result[:])
             for job in waiting:
                 quantise(*job)
             waiting = []

@@ -205,6 +205,12 @@ def tile_gatedcrossattention_pb_kernel(
         nc.tensor.transpose(bias_flipped[:, 0, 0:P], bias_rows_f32[:], identity[:])
         nc.vector.tensor_copy(out=bias_cols[:], in_=bias_flipped[:, 0, 0 : 2 * BLOCKS])
 
+        later_inputs = [
+            (path, quarter, group)
+            for quarter in range(1, QUARTERS)
+            for path in PATHS
+            for group in range(K_GROUPS)
+        ]
         activated = {}
         waiting = []
         for r in range(STEPS + 1):
@@ -230,9 +236,7 @@ def tile_gatedcrossattention_pb_kernel(
             for job in waiting:
                 quantise(*job)
             waiting = []
-            quarter, pair = divmod(r, QUARTER_STEPS)
-            if quarter + 1 < QUARTERS and pair in PATHS:
-                waiting = [
-                    features_onto_partitions(pair, quarter + 1, group, nc.scalar.copy)
-                    for group in range(K_GROUPS)
-                ]
+            waiting = [
+                features_onto_partitions(*job, nc.scalar.copy)
+                for job in (later_inputs[:2] if r == 0 else later_inputs[r + 1 : r + 2])
+            ]

@@ -56,6 +56,7 @@ def tile_gatedcrossattention_pb_kernel(
         stage = ctx.enter_context(tc.tile_pool(name="stage", bufs=4))
         turned = ctx.enter_context(tc.tile_pool(name="turned", bufs=3))
         blend = ctx.enter_context(tc.tile_pool(name="blend", bufs=2))
+        split = ctx.enter_context(tc.tile_pool(name="split", bufs=3))
         results = ctx.enter_context(tc.tile_pool(name="results", bufs=4))
         psum_in = ctx.enter_context(tc.psum_pool(name="psum_in", bufs=2))
         psum_mx = ctx.enter_context(tc.psum_pool(name="psum_mx", bufs=1))
@@ -100,16 +101,28 @@ def tile_gatedcrossattention_pb_kernel(
                     out=w_codes[path][:, :, cols].bitcast(I32), in_=w_codes_dram[path][:, :, cols]
                 )
 
-        def features_onto_partitions(path, quarter, group, copy):
+        def split_words(path, quarter):
+            slots = slice(quarter * QUARTER_SLOTS, (quarter + 1) * QUARTER_SLOTS)
+            sorted_words = split.tile([P, QUARTER_SLOTS, K_GROUPS, 2, P], F32, name="sorted_words")
+            nc.vector.tensor_copy(
+                out=sorted_words[:],
+                in_=rows[path][:, slots, :]
+                .rearrange("p s e -> p (s e)")
+                .bitcast(F32)
+                .rearrange("p (s g w h) -> p s g h w", s=QUARTER_SLOTS, g=K_GROUPS, h=2),
+            )
+            return sorted_words
+
+        def features_onto_partitions(path, quarter, group, copy, sorted_words=None):
             flipped = psum_in.tile([P, 2, QUARTER_TOKENS], F32, name="flipped")
             for h in range(2):
                 for j in range(QUARTER_SLOTS):
-                    words = rows[path][:, quarter * QUARTER_SLOTS + j, :].bitcast(F32)
-                    nc.tensor.transpose(
-                        flipped[:, h, j * P : (j + 1) * P],
-                        words[:, group * WORDS + h : (group + 1) * WORDS : 2],
-                        identity[:],
-                    )
+                    if sorted_words is None:
+                        words = rows[path][:, quarter * QUARTER_SLOTS + j, :].bitcast(F32)
+                        words = words[:, group * WORDS + h : (group + 1) * WORDS : 2]
+                    else:
+                        words = sorted_words[:, j, group, h, :]
+                    nc.tensor.transpose(flipped[:, h, j * P : (j + 1) * P], words, identity[:])
             grouped = stage.tile([P, 4 * QUARTER_TOKENS], BF16, align_bytes=64, name="grouped")
             copy(
                 out=grouped[:].bitcast(F32).rearrange("p (c h) -> p c h", h=2),
@@ -213,9 +226,18 @@ def tile_gatedcrossattention_pb_kernel(
         ]
         activated = {}
         waiting = []
+        sorted_words = {}
+        later_paths = [(path, quarter) for quarter in range(1, QUARTERS) for path in PATHS]
+        for path, quarter in later_paths[:1]:
+            sorted_words[path, quarter] = split_words(path, quarter)
         for r in range(STEPS + 1):
             if r < STEPS:
                 activated[r] = project(r)
+            for job in waiting:
+                quantise(*job)
+            if r % 2 == 0 and r // 2 + 1 < len(later_paths):
+                path, quarter = later_paths[r // 2 + 1]
+                sorted_words[path, quarter] = split_words(path, quarter)
             if 1 <= r <= STEPS:
                 u_t, c_t = activated[r - 1]
                 c_back = tokens_onto_partitions(CANDIDATE, c_t)
@@ -233,10 +255,8 @@ def tile_gatedcrossattention_pb_kernel(
                     out=result[:], in0=product[:], in1=step_view(rows[GATE], r - 1), op=ALU.add
                 )
                 nc.sync.dma_start(out=step_view(out_dram, r - 1), in_=result[:])
-            for job in waiting:
-                quantise(*job)
             waiting = []
             waiting = [
-                features_onto_partitions(*job, nc.scalar.copy)
+                features_onto_partitions(*job, nc.scalar.copy, sorted_words[job[:2]])
                 for job in (later_inputs[:2] if r == 0 else later_inputs[r + 1 : r + 2])
             ]

@@ -54,8 +54,8 @@ def tile_gatedcrossattention_pb_kernel(
     with ExitStack() as ctx:
         keep = ctx.enter_context(tc.tile_pool(name="keep", bufs=1))
         stage = ctx.enter_context(tc.tile_pool(name="stage", bufs=4))
-        turned = ctx.enter_context(tc.tile_pool(name="turned", bufs=3))
-        blend = ctx.enter_context(tc.tile_pool(name="blend", bufs=2))
+        turned = ctx.enter_context(tc.tile_pool(name="turned", bufs=4))
+        blend = ctx.enter_context(tc.tile_pool(name="blend", bufs=3))
         split = ctx.enter_context(tc.tile_pool(name="split", bufs=3))
         results = ctx.enter_context(tc.tile_pool(name="results", bufs=4))
         psum_in = ctx.enter_context(tc.psum_pool(name="psum_in", bufs=2))
@@ -71,7 +71,10 @@ def tile_gatedcrossattention_pb_kernel(
             keep.tile([P, K_GROUPS, FEATURES], U32, align_bytes=64, name="w_codes_" + PATH_NAMES[path])
             for path in PATHS
         ]
-        w_planes = keep.tile([P, FEATURES], U8, align_bytes=64)
+        w_planes = [
+            keep.tile([P, FEATURES], U8, align_bytes=64, name="w_planes_" + PATH_NAMES[path])
+            for path in PATHS
+        ]
         x_codes = keep.tile([P, 2, QUARTERS, K_GROUPS, QUARTER_TOKENS], U32, align_bytes=64)
         x_planes = keep.tile([P, 2, QUARTERS, K_GROUPS, QUARTER_TOKENS], U8, align_bytes=64)
         identity = keep.tile([P, P], F32)
@@ -79,27 +82,25 @@ def tile_gatedcrossattention_pb_kernel(
         bias_rows_f32 = keep.tile([P, P], F32)
         bias_cols = keep.tile([P, 2 * BLOCKS], F32)
         table_warmer = keep.tile([P, 1], F32)
+        zeros = keep.tile([P, 4 * P], BF16)
 
-        def load_rows(quarter):
+        def load_rows(path, quarter):
             slots = slice(quarter * QUARTER_SLOTS, (quarter + 1) * QUARTER_SLOTS)
-            for path in PATHS:
-                nc.sync.dma_start(out=rows[path][:, slots, :], in_=rows_dram[path][:, slots, :])
+            nc.sync.dma_start(out=rows[path][:, slots, :], in_=rows_dram[path][:, slots, :])
 
-        def load_weight_scales():
-            for path in PATHS:
-                for quadrant in range(4):
-                    first = 32 * quadrant + 4 * K_GROUPS * path
-                    nc.sync.dma_start(
-                        out=w_planes[first : first + 4 * K_GROUPS, :].bitcast(I32),
-                        in_=w_scales_dram[path][:, 4 * quadrant : 4 * quadrant + 4, :].bitcast(I32),
-                    )
-
-        def load_weights(pair):
-            cols = slice(pair * STEP_FEATURES, (pair + 1) * STEP_FEATURES)
-            for path in PATHS:
+        def load_weight_scales(path):
+            for quadrant in range(4):
+                first = 32 * quadrant
                 nc.sync.dma_start(
-                    out=w_codes[path][:, :, cols].bitcast(I32), in_=w_codes_dram[path][:, :, cols]
+                    out=w_planes[path][first : first + 4 * K_GROUPS, :].bitcast(I32),
+                    in_=w_scales_dram[path][:, 4 * quadrant : 4 * quadrant + 4, :].bitcast(I32),
                 )
+
+        def load_weights(path, pair):
+            cols = slice(pair * STEP_FEATURES, (pair + 1) * STEP_FEATURES)
+            nc.sync.dma_start(
+                out=w_codes[path][:, :, cols].bitcast(I32), in_=w_codes_dram[path][:, :, cols]
+            )
 
         def split_words(path, quarter):
             slots = slice(quarter * QUARTER_SLOTS, (quarter + 1) * QUARTER_SLOTS)
@@ -113,8 +114,9 @@ def tile_gatedcrossattention_pb_kernel(
             )
             return sorted_words
 
-        def features_onto_partitions(path, quarter, group, copy, sorted_words=None):
-            flipped = psum_in.tile([P, 2, QUARTER_TOKENS], F32, name="flipped")
+        def features_onto_partitions(path, quarter, group, copy, sorted_words=None, flipped=None):
+            if flipped is None:
+                flipped = psum_in.tile([P, 2, QUARTER_TOKENS], F32, name="flipped")
             for h in range(2):
                 for j in range(QUARTER_SLOTS):
                     if sorted_words is None:
@@ -137,58 +139,83 @@ def tile_gatedcrossattention_pb_kernel(
                 in_=grouped[:],
             )
 
-        def project(step):
+        def project(path, step):
             quarter, pair = divmod(step, QUARTER_STEPS)
-            activated = []
-            for path in PATHS:
-                acc = psum_mx.tile([P, STEP_BLOCKS, QUARTER_TOKENS], F32, name="acc_" + PATH_NAMES[path])
-                for j in range(STEP_BLOCKS):
-                    block = pair * STEP_BLOCKS + j
-                    cols = slice(block * P, (block + 1) * P)
-                    for group in range(K_GROUPS):
-                        plane_start = 4 * (K_GROUPS * path + group)
-                        nc.tensor.matmul_mx(
-                            out=acc[:, j, :],
-                            lhsT=w_codes[path][:, group, cols].bitcast(FP8X4),
-                            lhsT_scale=w_planes[plane_start:P, cols],
-                            rhs=x_codes[:, path, quarter, group, :].bitcast(FP8X4),
-                            rhs_scale=x_planes[:, path, quarter, group, :],
-                            start=(group == 0),
-                            stop=(group == K_GROUPS - 1),
-                        )
-                value = turned.tile([P, STEP_BLOCKS, QUARTER_TOKENS], F32, name="turned_" + PATH_NAMES[path])
-                for j in range(STEP_BLOCKS):
-                    column = path * BLOCKS + pair * STEP_BLOCKS + j
-                    nc.scalar.activation(
-                        out=value[:, j, :],
-                        in_=acc[:, j, :],
-                        func=FUNCTIONS[path],
-                        bias=bias_cols[:, column : column + 1],
-                        scale=1.0,
+            acc = psum_mx.tile([P, STEP_BLOCKS, QUARTER_TOKENS], F32, name="acc_" + PATH_NAMES[path])
+            value = turned.tile([P, STEP_BLOCKS, QUARTER_TOKENS], F32, name="turned_" + PATH_NAMES[path])
+            for j in range(STEP_BLOCKS):
+                block = pair * STEP_BLOCKS + j
+                cols = slice(block * P, (block + 1) * P)
+                for group in range(K_GROUPS):
+                    nc.tensor.matmul_mx(
+                        out=acc[:, j, :],
+                        lhsT=w_codes[path][:, group, cols].bitcast(FP8X4),
+                        lhsT_scale=w_planes[path][4 * group : P, cols],
+                        rhs=x_codes[:, path, quarter, group, :].bitcast(FP8X4),
+                        rhs_scale=x_planes[:, path, quarter, group, :],
+                        start=(group == 0),
+                        stop=(group == K_GROUPS - 1),
                     )
-                activated.append(value)
-            return activated
+            for j in range(STEP_BLOCKS):
+                column = path * BLOCKS + pair * STEP_BLOCKS + j
+                nc.scalar.activation(
+                    out=value[:, j, :],
+                    in_=acc[:, j, :],
+                    func=FUNCTIONS[path],
+                    bias=bias_cols[:, column : column + 1],
+                    scale=1.0,
+                )
+            return value
 
-        def tokens_onto_partitions(path, value):
-            back = psum_back.tile([P, QUARTER_SLOTS, STEP_FEATURES], F32, name="back_" + PATH_NAMES[path])
+        def tokens_onto_partitions(path, value, blocks):
+            back = psum_back.tile([P, QUARTER_SLOTS, len(blocks) * P], F32, name="back_" + PATH_NAMES[path])
             for s in range(QUARTER_SLOTS):
-                for j in range(STEP_BLOCKS):
+                for i, j in enumerate(blocks):
                     nc.tensor.transpose(
-                        back[:, s, j * P : (j + 1) * P], value[:, j, s * P : (s + 1) * P], identity[:]
+                        back[:, s, i * P : (i + 1) * P], value[:, j, s * P : (s + 1) * P], identity[:]
                     )
             return back
 
-        def step_view(tensor, step):
+        def step_view(tensor, step, blocks):
             quarter, pair = divmod(step, QUARTER_STEPS)
+            first = pair * STEP_FEATURES + blocks[0] * P
             return tensor[
                 :,
                 quarter * QUARTER_SLOTS : (quarter + 1) * QUARTER_SLOTS,
-                pair * STEP_FEATURES : (pair + 1) * STEP_FEATURES,
+                first : first + len(blocks) * P,
             ]
 
-        nc.vector.memset(w_planes[:].bitcast(I32), 0)
-        nc.vector.memset(bias_rows[:], 0.0)
+        def blend_and_store(step, pieces, adder):
+            shape = [P, QUARTER_SLOTS, len(pieces[0]) * P]
+            queries = [step_view(rows[GATE], step, blocks) for blocks in pieces]
+            backs = []
+            for blocks in pieces:
+                c_back = tokens_onto_partitions(CANDIDATE, c_values[step], blocks)
+                backs.append((tokens_onto_partitions(GATE, u_values[step], blocks), c_back))
+            differences, products = [], []
+            for (u_back, c_back), query in zip(backs, queries):
+                difference = blend.tile(shape, F32, name="difference")
+                nc.vector.tensor_tensor(out=difference[:], in0=c_back[:], in1=query, op=ALU.subtract)
+                differences.append(difference)
+            for (u_back, c_back), difference in zip(backs, differences):
+                product = blend.tile(shape, F32, name="product")
+                nc.vector.tensor_tensor(out=product[:], in0=u_back[:], in1=difference[:], op=ALU.mult)
+                products.append(product)
+            for blocks, query, product in zip(pieces, queries, products):
+                result = results.tile(shape, F32, name="result")
+                adder.tensor_tensor(out=result[:], in0=product[:], in1=query, op=ALU.add)
+                nc.sync.dma_start(out=step_view(out_dram, step, blocks), in_=result[:])
+
+        def keep_clock_up(passes):
+            unread = psum_back.tile([P, 4 * P], F32, name="back_" + PATH_NAMES[GATE])
+            for i in range(passes):
+                nc.tensor.matmul(unread[:], zeros[:, 0:P], zeros[:], start=True, stop=True)
+
+        nc.vector.memset(zeros[:], 0.0)
         nc.vector.memset(table_warmer[:], 0.0)
+        for path in PATHS:
+            nc.vector.memset(w_planes[path][:].bitcast(I32), 0)
+        nc.vector.memset(bias_rows[:], 0.0)
         for path in PATHS:
             nc.scalar.dma_start(
                 out=bias_rows[path * BLOCKS : (path + 1) * BLOCKS, :], in_=bias_dram[path]
@@ -196,67 +223,72 @@ def tile_gatedcrossattention_pb_kernel(
         nc.scalar.activation(out=table_warmer[:], in_=table_warmer[:], func=ACT.Sigmoid)
         make_identity(nc, identity[:])
 
-        load_rows(0)
-        load_weight_scales()
-        load_weights(0)
-        load_weights(1)
-        load_rows(1)
-        load_weights(2)
-        load_weights(3)
-        load_rows(2)
-        load_rows(3)
+        load_rows(GATE, 0)
+        load_weight_scales(GATE)
+        load_weights(GATE, 0)
+        load_rows(CANDIDATE, 0)
+        load_weights(GATE, 1)
+        load_weight_scales(CANDIDATE)
+        load_weights(CANDIDATE, 0)
+        load_weights(CANDIDATE, 1)
+        load_rows(GATE, 1)
+        load_weights(GATE, 2)
+        load_weights(CANDIDATE, 2)
+        load_rows(CANDIDATE, 1)
+        load_weights(GATE, 3)
+        load_weights(CANDIDATE, 3)
+        for quarter in range(2, QUARTERS):
+            for path in PATHS:
+                load_rows(path, quarter)
 
-        nc.vector.tensor_copy(out=bias_rows_f32[:], in_=bias_rows[:])
-        for path in PATHS:
-            jobs = [
-                features_onto_partitions(path, 0, 0, nc.vector.tensor_copy),
-                features_onto_partitions(path, 0, 1, nc.scalar.copy),
+        def first_quarter(path):
+            banks = [None, None]
+            if path == CANDIDATE:
+                banks = [
+                    psum_back.tile([P, 2, QUARTER_TOKENS], F32, name="back_" + PATH_NAMES[CANDIDATE])
+                    for group in range(K_GROUPS)
+                ]
+            return [
+                features_onto_partitions(path, 0, 0, nc.vector.tensor_copy, None, banks[0]),
+                features_onto_partitions(path, 0, 1, nc.scalar.copy, None, banks[1]),
             ]
-            for job in jobs:
-                quantise(*job)
+
+        u_values, c_values = {}, {}
+        nc.vector.tensor_copy(out=bias_rows_f32[:], in_=bias_rows[:])
+        keep_clock_up(6)
+        first = first_quarter(GATE)
         bias_flipped = psum_in.tile([P, 2, QUARTER_TOKENS], F32, name="flipped")
         nc.tensor.transpose(bias_flipped[:, 0, 0:P], bias_rows_f32[:], identity[:])
+        keep_clock_up(3)
+        for job in first:
+            quantise(*job)
         nc.vector.tensor_copy(out=bias_cols[:], in_=bias_flipped[:, 0, 0 : 2 * BLOCKS])
+        u_values[0] = project(GATE, 0)
+        first = first_quarter(CANDIDATE)
+        for job in first:
+            quantise(*job)
+        u_values[1] = project(GATE, 1)
 
-        later_inputs = [
-            (path, quarter, group)
-            for quarter in range(1, QUARTERS)
-            for path in PATHS
-            for group in range(K_GROUPS)
-        ]
-        activated = {}
-        waiting = []
-        sorted_words = {}
         later_paths = [(path, quarter) for quarter in range(1, QUARTERS) for path in PATHS]
-        for path, quarter in later_paths[:1]:
-            sorted_words[path, quarter] = split_words(path, quarter)
-        for r in range(STEPS + 1):
-            if r < STEPS:
-                activated[r] = project(r)
+        later_inputs = [(path, quarter, group) for path, quarter in later_paths for group in range(K_GROUPS)]
+        sorted_words = {}
+        waiting = []
+        for r in range(STEPS):
+            if r not in u_values:
+                u_values[r] = project(GATE, r)
+            if r < STEPS - 1:
+                c_values[r] = project(CANDIDATE, r)
             for job in waiting:
                 quantise(*job)
-            if r % 2 == 0 and r // 2 + 1 < len(later_paths):
-                path, quarter = later_paths[r // 2 + 1]
-                sorted_words[path, quarter] = split_words(path, quarter)
-            if 1 <= r <= STEPS:
-                u_t, c_t = activated[r - 1]
-                c_back = tokens_onto_partitions(CANDIDATE, c_t)
-                u_back = tokens_onto_partitions(GATE, u_t)
-                difference = blend.tile([P, QUARTER_SLOTS, STEP_FEATURES], F32, name="difference")
-                nc.vector.tensor_tensor(
-                    out=difference[:], in0=c_back[:], in1=step_view(rows[GATE], r - 1), op=ALU.subtract
-                )
-                product = blend.tile([P, QUARTER_SLOTS, STEP_FEATURES], F32, name="product")
-                nc.vector.tensor_tensor(
-                    out=product[:], in0=u_back[:], in1=difference[:], op=ALU.mult
-                )
-                result = results.tile([P, QUARTER_SLOTS, STEP_FEATURES], F32, name="result")
-                nc.gpsimd.tensor_tensor(
-                    out=result[:], in0=product[:], in1=step_view(rows[GATE], r - 1), op=ALU.add
-                )
-                nc.sync.dma_start(out=step_view(out_dram, r - 1), in_=result[:])
             waiting = []
+            if r % 2 == 0 and 0 < r // 2 + 1 < len(later_paths):
+                key = later_paths[r // 2 + 1]
+                sorted_words[key] = split_words(*key)
+            if r >= 1:
+                blend_and_store(r - 1, [[0, 1]], nc.gpsimd)
             waiting = [
-                features_onto_partitions(*job, nc.scalar.copy, sorted_words[job[:2]])
+                features_onto_partitions(*job, nc.scalar.copy, sorted_words.get(job[:2]))
                 for job in (later_inputs[:2] if r == 0 else later_inputs[r + 1 : r + 2])
             ]
+        c_values[STEPS - 1] = project(CANDIDATE, STEPS - 1)
+        blend_and_store(STEPS - 1, [[0], [1]], nc.vector)

@@ -85,7 +85,9 @@ def tile_gatedcrossattention_pb_kernel(
         zeros = keep.tile([P, 4 * P], BF16)
 
         def load_rows(path, quarter):
-            slots = slice(quarter * QUARTER_SLOTS, (quarter + 1) * QUARTER_SLOTS)
+            load_slots(path, slice(quarter * QUARTER_SLOTS, (quarter + 1) * QUARTER_SLOTS))
+
+        def load_slots(path, slots):
             nc.sync.dma_start(out=rows[path][:, slots, :], in_=rows_dram[path][:, slots, :])
 
         def load_weight_scales(path):
@@ -132,6 +134,34 @@ def tile_gatedcrossattention_pb_kernel(
             )
             return (path, quarter, group, grouped)
 
+        def slot_onto_partitions(path, slot, copy, flipped=None):
+            if flipped is None:
+                flipped = psum_in.tile([P, 2, QUARTER_TOKENS], F32, name="flipped")
+            turned_words = flipped[:].rearrange("p g (h c) -> p g h c", h=2)
+            words = rows[path][:, slot, :].bitcast(F32)
+            for group in range(K_GROUPS):
+                for h in range(2):
+                    nc.tensor.transpose(
+                        turned_words[:, group, h, :],
+                        words[:, group * WORDS + h : (group + 1) * WORDS : 2],
+                        identity[:],
+                    )
+            grouped = stage.tile([P, 4 * QUARTER_TOKENS], BF16, align_bytes=64, name="grouped")
+            copy(
+                out=grouped[:].bitcast(F32).rearrange("p (g c h) -> p g c h", g=K_GROUPS, h=2),
+                in_=turned_words.rearrange("p g h c -> p g c h"),
+            )
+            return (path, slot, grouped)
+
+        def quantise_slot(path, slot, grouped):
+            tokens = slice(slot * P, (slot + 1) * P)
+            for group in range(K_GROUPS):
+                nc.vector.quantize_mx(
+                    out=x_codes[:, path, 0, group, tokens].bitcast(FP8X4),
+                    scales=x_planes[:, path, 0, group, tokens],
+                    in_=grouped[:, group * K_PASS : (group + 1) * K_PASS],
+                )
+
         def quantise(path, quarter, group, grouped):
             nc.vector.quantize_mx(
                 out=x_codes[:, path, quarter, group, :].bitcast(FP8X4),
@@ -139,9 +169,10 @@ def tile_gatedcrossattention_pb_kernel(
                 in_=grouped[:],
             )
 
-        def project(path, step):
+        def project(path, step, acc=None):
             quarter, pair = divmod(step, QUARTER_STEPS)
-            acc = psum_mx.tile([P, STEP_BLOCKS, QUARTER_TOKENS], F32, name="acc_" + PATH_NAMES[path])
+            if acc is None:
+                acc = psum_mx.tile([P, STEP_BLOCKS, QUARTER_TOKENS], F32, name="acc_" + PATH_NAMES[path])
             value = turned.tile([P, STEP_BLOCKS, QUARTER_TOKENS], F32, name="turned_" + PATH_NAMES[path])
             for j in range(STEP_BLOCKS):
                 block = pair * STEP_BLOCKS + j
@@ -167,8 +198,8 @@ def tile_gatedcrossattention_pb_kernel(
                 )
             return value
 
-        def tokens_onto_partitions(path, value, blocks):
-            back = psum_back.tile([P, QUARTER_SLOTS, len(blocks) * P], F32, name="back_" + PATH_NAMES[path])
+        def tokens_onto_partitions(path, value, blocks, pool):
+            back = pool.tile([P, QUARTER_SLOTS, len(blocks) * P], F32, name="flipped" if pool is psum_in else "back_" + PATH_NAMES[path])
             for s in range(QUARTER_SLOTS):
                 for i, j in enumerate(blocks):
                     nc.tensor.transpose(
@@ -185,18 +216,23 @@ def tile_gatedcrossattention_pb_kernel(
                 first : first + len(blocks) * P,
             ]
 
-        def blend_and_store(step, pieces, adder):
+        def blend_and_store(step, pieces, adder, last=False, key=None, u_back=None):
             shape = [P, QUARTER_SLOTS, len(pieces[0]) * P]
             queries = [step_view(rows[GATE], step, blocks) for blocks in pieces]
             backs = []
             for blocks in pieces:
-                c_back = tokens_onto_partitions(CANDIDATE, c_values[step], blocks)
-                backs.append((tokens_onto_partitions(GATE, u_values[step], blocks), c_back))
+                pool = psum_in if last and blocks[0] == 0 else psum_back
+                c_back = tokens_onto_partitions(CANDIDATE, c_values[step], blocks, pool)
+                if u_back is None or blocks[0]:
+                    u_back = tokens_onto_partitions(GATE, u_values[step], blocks, pool)
+                backs.append((u_back, c_back))
             differences, products = [], []
             for (u_back, c_back), query in zip(backs, queries):
                 difference = blend.tile(shape, F32, name="difference")
                 nc.vector.tensor_tensor(out=difference[:], in0=c_back[:], in1=query, op=ALU.subtract)
                 differences.append(difference)
+            if key is not None:
+                sorted_words[key] = split_words(*key)
             for (u_back, c_back), difference in zip(backs, differences):
                 product = blend.tile(shape, F32, name="product")
                 nc.vector.tensor_tensor(out=product[:], in0=u_back[:], in1=difference[:], op=ALU.mult)
@@ -223,10 +259,11 @@ def tile_gatedcrossattention_pb_kernel(
         nc.scalar.activation(out=table_warmer[:], in_=table_warmer[:], func=ACT.Sigmoid)
         make_identity(nc, identity[:])
 
-        load_rows(GATE, 0)
+        for slot in range(QUARTER_SLOTS):
+            load_slots(GATE, slice(slot, slot + 1))
+        load_rows(CANDIDATE, 0)
         load_weight_scales(GATE)
         load_weights(GATE, 0)
-        load_rows(CANDIDATE, 0)
         load_weights(GATE, 1)
         load_weight_scales(CANDIDATE)
         load_weights(CANDIDATE, 0)
@@ -246,49 +283,50 @@ def tile_gatedcrossattention_pb_kernel(
             if path == CANDIDATE:
                 banks = [
                     psum_back.tile([P, 2, QUARTER_TOKENS], F32, name="back_" + PATH_NAMES[CANDIDATE])
-                    for group in range(K_GROUPS)
+                    for slot in range(QUARTER_SLOTS)
                 ]
             return [
-                features_onto_partitions(path, 0, 0, nc.vector.tensor_copy, None, banks[0]),
-                features_onto_partitions(path, 0, 1, nc.scalar.copy, None, banks[1]),
+                slot_onto_partitions(path, 0, nc.vector.tensor_copy, banks[0]),
+                slot_onto_partitions(path, 1, nc.scalar.copy, banks[1]),
             ]
 
         u_values, c_values = {}, {}
-        nc.vector.tensor_copy(out=bias_rows_f32[:], in_=bias_rows[:])
-        keep_clock_up(6)
+        nc.gpsimd.tensor_copy(out=bias_rows_f32[:], in_=bias_rows[:])
+        keep_clock_up(5)
         first = first_quarter(GATE)
-        bias_flipped = psum_in.tile([P, 2, QUARTER_TOKENS], F32, name="flipped")
-        nc.tensor.transpose(bias_flipped[:, 0, 0:P], bias_rows_f32[:], identity[:])
         keep_clock_up(3)
         for job in first:
-            quantise(*job)
+            quantise_slot(*job)
+        first = first_quarter(CANDIDATE)
+        bias_flipped = psum_in.tile([P, 2, QUARTER_TOKENS], F32, name="flipped")
+        nc.tensor.transpose(bias_flipped[:, 0, 0:P], bias_rows_f32[:], identity[:])
         nc.vector.tensor_copy(out=bias_cols[:], in_=bias_flipped[:, 0, 0 : 2 * BLOCKS])
         u_values[0] = project(GATE, 0)
-        first = first_quarter(CANDIDATE)
         for job in first:
-            quantise(*job)
-        u_values[1] = project(GATE, 1)
+            quantise_slot(*job)
+        u_values[1] = project(GATE, 1, psum_in.tile([P, 2, QUARTER_TOKENS], F32, name="flipped"))
+        c_values[0] = project(CANDIDATE, 0)
+        c_values[1] = project(CANDIDATE, 1, psum_back.tile([P, 2, QUARTER_TOKENS], F32, name="back_" + PATH_NAMES[GATE]))
 
         later_paths = [(path, quarter) for quarter in range(1, QUARTERS) for path in PATHS]
         later_inputs = [(path, quarter, group) for path, quarter in later_paths for group in range(K_GROUPS)]
         sorted_words = {}
         waiting = []
-        for r in range(STEPS):
-            if r not in u_values:
+        for r in range(1, STEPS):
+            if r >= 2:
                 u_values[r] = project(GATE, r)
-            if r < STEPS - 1:
                 c_values[r] = project(CANDIDATE, r)
             for job in waiting:
                 quantise(*job)
-            waiting = []
-            if r % 2 == 0 and 0 < r // 2 + 1 < len(later_paths):
-                key = later_paths[r // 2 + 1]
-                sorted_words[key] = split_words(*key)
-            if r >= 1:
-                blend_and_store(r - 1, [[0, 1]], nc.gpsimd)
-            waiting = [
-                features_onto_partitions(*job, nc.scalar.copy, sorted_words.get(job[:2]))
-                for job in (later_inputs[:2] if r == 0 else later_inputs[r + 1 : r + 2])
-            ]
-        c_values[STEPS - 1] = project(CANDIDATE, STEPS - 1)
-        blend_and_store(STEPS - 1, [[0], [1]], nc.vector)
+            jobs = later_inputs[0:2] if r == 1 else later_inputs[2:4] if r == 2 else later_inputs[r + 1 : r + 2]
+            early = r == 1
+            if early:
+                early_u = tokens_onto_partitions(GATE, u_values[0], [0, 1], psum_back)
+                waiting = [features_onto_partitions(*job, nc.scalar.copy, sorted_words.get(job[:2])) for job in jobs]
+            key = None
+            if r == 1 or (r % 2 == 0 and r // 2 + 1 < len(later_paths)):
+                key = later_paths[1 if r == 1 else r // 2 + 1]
+            blend_and_store(r - 1, [[0, 1]], nc.gpsimd, key=key, u_back=early_u if r == 1 else None)
+            if not early:
+                waiting = [features_onto_partitions(*job, nc.scalar.copy, sorted_words.get(job[:2])) for job in jobs]
+        blend_and_store(STEPS - 1, [[0], [1]], nc.vector, last=True)

@@ -78,16 +78,14 @@ def tile_gatedcrossattention_pb_kernel(
         x_codes = keep.tile([P, 2, QUARTERS, K_GROUPS, QUARTER_TOKENS], U32, align_bytes=64)
         x_planes = keep.tile([P, 2, QUARTERS, K_GROUPS, QUARTER_TOKENS], U8, align_bytes=64)
         identity = keep.tile([P, P], F32)
-        bias_rows = keep.tile([P, P], BF16)
-        bias_rows_f32 = keep.tile([P, P], F32)
-        bias_cols = keep.tile([P, 2 * BLOCKS], F32)
+        bias_rows = [keep.tile([P, P], BF16, name="bias_rows_" + PATH_NAMES[path]) for path in PATHS]
+        bias_rows_f32 = [keep.tile([P, P], F32, name="bias_f32_" + PATH_NAMES[path]) for path in PATHS]
+        bias_cols = [keep.tile([P, BLOCKS], F32, name="bias_cols_" + PATH_NAMES[path]) for path in PATHS]
         table_warmer = keep.tile([P, 1], F32)
-        zeros = keep.tile([P, 4 * P], BF16)
+        zeros = keep.tile([P, 2 * P], BF16)
 
         def load_rows(path, quarter):
-            load_slots(path, slice(quarter * QUARTER_SLOTS, (quarter + 1) * QUARTER_SLOTS))
-
-        def load_slots(path, slots):
+            slots = slice(quarter * QUARTER_SLOTS, (quarter + 1) * QUARTER_SLOTS)
             nc.sync.dma_start(out=rows[path][:, slots, :], in_=rows_dram[path][:, slots, :])
 
         def load_weight_scales(path):
@@ -134,34 +132,6 @@ def tile_gatedcrossattention_pb_kernel(
             )
             return (path, quarter, group, grouped)
 
-        def slot_onto_partitions(path, slot, copy, flipped=None):
-            if flipped is None:
-                flipped = psum_in.tile([P, 2, QUARTER_TOKENS], F32, name="flipped")
-            turned_words = flipped[:].rearrange("p g (h c) -> p g h c", h=2)
-            words = rows[path][:, slot, :].bitcast(F32)
-            for group in range(K_GROUPS):
-                for h in range(2):
-                    nc.tensor.transpose(
-                        turned_words[:, group, h, :],
-                        words[:, group * WORDS + h : (group + 1) * WORDS : 2],
-                        identity[:],
-                    )
-            grouped = stage.tile([P, 4 * QUARTER_TOKENS], BF16, align_bytes=64, name="grouped")
-            copy(
-                out=grouped[:].bitcast(F32).rearrange("p (g c h) -> p g c h", g=K_GROUPS, h=2),
-                in_=turned_words.rearrange("p g h c -> p g c h"),
-            )
-            return (path, slot, grouped)
-
-        def quantise_slot(path, slot, grouped):
-            tokens = slice(slot * P, (slot + 1) * P)
-            for group in range(K_GROUPS):
-                nc.vector.quantize_mx(
-                    out=x_codes[:, path, 0, group, tokens].bitcast(FP8X4),
-                    scales=x_planes[:, path, 0, group, tokens],
-                    in_=grouped[:, group * K_PASS : (group + 1) * K_PASS],
-                )
-
         def quantise(path, quarter, group, grouped):
             nc.vector.quantize_mx(
                 out=x_codes[:, path, quarter, group, :].bitcast(FP8X4),
@@ -169,11 +139,10 @@ def tile_gatedcrossattention_pb_kernel(
                 in_=grouped[:],
             )
 
-        def project(path, step, acc=None):
+        def multiply(path, step, acc=None):
             quarter, pair = divmod(step, QUARTER_STEPS)
             if acc is None:
                 acc = psum_mx.tile([P, STEP_BLOCKS, QUARTER_TOKENS], F32, name="acc_" + PATH_NAMES[path])
-            value = turned.tile([P, STEP_BLOCKS, QUARTER_TOKENS], F32, name="turned_" + PATH_NAMES[path])
             for j in range(STEP_BLOCKS):
                 block = pair * STEP_BLOCKS + j
                 cols = slice(block * P, (block + 1) * P)
@@ -187,16 +156,24 @@ def tile_gatedcrossattention_pb_kernel(
                         start=(group == 0),
                         stop=(group == K_GROUPS - 1),
                     )
+            return acc
+
+        def activate(path, step, acc):
+            value = turned.tile([P, STEP_BLOCKS, QUARTER_TOKENS], F32, name="turned_" + PATH_NAMES[path])
+            first_column = step % QUARTER_STEPS * STEP_BLOCKS
             for j in range(STEP_BLOCKS):
-                column = path * BLOCKS + pair * STEP_BLOCKS + j
+                column = first_column + j
                 nc.scalar.activation(
                     out=value[:, j, :],
                     in_=acc[:, j, :],
                     func=FUNCTIONS[path],
-                    bias=bias_cols[:, column : column + 1],
+                    bias=bias_cols[path][:, column : column + 1],
                     scale=1.0,
                 )
             return value
+
+        def project(path, step, acc=None):
+            return activate(path, step, multiply(path, step, acc))
 
         def tokens_onto_partitions(path, value, blocks, pool):
             back = pool.tile([P, QUARTER_SLOTS, len(blocks) * P], F32, name="flipped" if pool is psum_in else "back_" + PATH_NAMES[path])
@@ -243,27 +220,33 @@ def tile_gatedcrossattention_pb_kernel(
                 nc.sync.dma_start(out=step_view(out_dram, step, blocks), in_=result[:])
 
         def keep_clock_up(passes):
-            unread = psum_back.tile([P, 4 * P], F32, name="back_" + PATH_NAMES[GATE])
+            unread = psum_back.tile([P, 2, QUARTER_TOKENS], F32, name="back_" + PATH_NAMES[GATE])
             for i in range(passes):
-                nc.tensor.matmul(unread[:], zeros[:, 0:P], zeros[:], start=True, stop=True)
+                nc.tensor.matmul(unread[:, 0, :], zeros[:, 0:P], zeros[:], start=True, stop=True)
 
-        nc.vector.memset(zeros[:], 0.0)
+        def load_bias(path):
+            nc.scalar.dma_start(out=bias_rows[path][0:BLOCKS, :], in_=bias_dram[path])
+
+        def bias_onto_partitions(path):
+            flipped = psum_back.tile([P, 2, QUARTER_TOKENS], F32, name="back_" + PATH_NAMES[GATE])
+            nc.tensor.transpose(flipped[:, 0, 0:P], bias_rows_f32[path][:], identity[:])
+            nc.vector.tensor_copy(out=bias_cols[path][:], in_=flipped[:, 0, 0:BLOCKS])
+
+        nc.vector.memset(bias_rows[GATE][:], 0.0)
+        nc.vector.memset(w_planes[GATE][:].bitcast(I32), 0)
         nc.vector.memset(table_warmer[:], 0.0)
-        for path in PATHS:
-            nc.vector.memset(w_planes[path][:].bitcast(I32), 0)
-        nc.vector.memset(bias_rows[:], 0.0)
-        for path in PATHS:
-            nc.scalar.dma_start(
-                out=bias_rows[path * BLOCKS : (path + 1) * BLOCKS, :], in_=bias_dram[path]
-            )
+        nc.vector.memset(zeros[:], 0.0)
+        nc.vector.memset(bias_rows[CANDIDATE][:], 0.0)
+        nc.vector.memset(w_planes[CANDIDATE][:].bitcast(I32), 0)
         nc.scalar.activation(out=table_warmer[:], in_=table_warmer[:], func=ACT.Sigmoid)
         make_identity(nc, identity[:])
 
-        for slot in range(QUARTER_SLOTS):
-            load_slots(GATE, slice(slot, slot + 1))
-        load_rows(CANDIDATE, 0)
+        load_rows(GATE, 0)
         load_weight_scales(GATE)
         load_weights(GATE, 0)
+        load_rows(CANDIDATE, 0)
+        load_bias(GATE)
+        load_bias(CANDIDATE)
         load_weights(GATE, 1)
         load_weight_scales(CANDIDATE)
         load_weights(CANDIDATE, 0)
@@ -283,28 +266,28 @@ def tile_gatedcrossattention_pb_kernel(
             if path == CANDIDATE:
                 banks = [
                     psum_back.tile([P, 2, QUARTER_TOKENS], F32, name="back_" + PATH_NAMES[CANDIDATE])
-                    for slot in range(QUARTER_SLOTS)
+                    for group in range(K_GROUPS)
                 ]
             return [
-                slot_onto_partitions(path, 0, nc.vector.tensor_copy, banks[0]),
-                slot_onto_partitions(path, 1, nc.scalar.copy, banks[1]),
+                features_onto_partitions(path, 0, 0, nc.vector.tensor_copy, None, banks[0]),
+                features_onto_partitions(path, 0, 1, nc.scalar.copy, None, banks[1]),
             ]
 
         u_values, c_values = {}, {}
-        nc.gpsimd.tensor_copy(out=bias_rows_f32[:], in_=bias_rows[:])
-        keep_clock_up(5)
+        for path in PATHS:
+            nc.gpsimd.tensor_copy(out=bias_rows_f32[path][:], in_=bias_rows[path][:])
+        keep_clock_up(9)
         first = first_quarter(GATE)
-        keep_clock_up(3)
+        keep_clock_up(4)
         for job in first:
-            quantise_slot(*job)
+            quantise(*job)
         first = first_quarter(CANDIDATE)
-        bias_flipped = psum_in.tile([P, 2, QUARTER_TOKENS], F32, name="flipped")
-        nc.tensor.transpose(bias_flipped[:, 0, 0:P], bias_rows_f32[:], identity[:])
-        nc.vector.tensor_copy(out=bias_cols[:], in_=bias_flipped[:, 0, 0 : 2 * BLOCKS])
+        bias_onto_partitions(GATE)
         u_values[0] = project(GATE, 0)
         for job in first:
-            quantise_slot(*job)
+            quantise(*job)
         u_values[1] = project(GATE, 1, psum_in.tile([P, 2, QUARTER_TOKENS], F32, name="flipped"))
+        bias_onto_partitions(CANDIDATE)
         c_values[0] = project(CANDIDATE, 0)
         c_values[1] = project(CANDIDATE, 1, psum_back.tile([P, 2, QUARTER_TOKENS], F32, name="back_" + PATH_NAMES[GATE]))
 
@@ -315,18 +298,20 @@ def tile_gatedcrossattention_pb_kernel(
         for r in range(1, STEPS):
             if r >= 2:
                 u_values[r] = project(GATE, r)
-                c_values[r] = project(CANDIDATE, r)
+                if r < STEPS - 1:
+                    c_values[r] = project(CANDIDATE, r)
             for job in waiting:
                 quantise(*job)
+            if r % 2 == 0 and r // 2 + 1 < len(later_paths):
+                sorted_words[later_paths[r // 2 + 1]] = split_words(*later_paths[r // 2 + 1])
             jobs = later_inputs[0:2] if r == 1 else later_inputs[2:4] if r == 2 else later_inputs[r + 1 : r + 2]
             early = r == 1
             if early:
                 early_u = tokens_onto_partitions(GATE, u_values[0], [0, 1], psum_back)
                 waiting = [features_onto_partitions(*job, nc.scalar.copy, sorted_words.get(job[:2])) for job in jobs]
-            key = None
-            if r == 1 or (r % 2 == 0 and r // 2 + 1 < len(later_paths)):
-                key = later_paths[1 if r == 1 else r // 2 + 1]
+            key = later_paths[1] if r == 1 else None
             blend_and_store(r - 1, [[0, 1]], nc.gpsimd, key=key, u_back=early_u if r == 1 else None)
             if not early:
                 waiting = [features_onto_partitions(*job, nc.scalar.copy, sorted_words.get(job[:2])) for job in jobs]
+        c_values[STEPS - 1] = project(CANDIDATE, STEPS - 1)
         blend_and_store(STEPS - 1, [[0], [1]], nc.vector, last=True)

@@ -193,23 +193,19 @@ def tile_gatedcrossattention_pb_kernel(
                 first : first + len(blocks) * P,
             ]
 
-        def blend_and_store(step, pieces, adder, last=False, key=None, u_back=None):
+        def blend_and_store(step, pieces, adder, last=False):
             shape = [P, QUARTER_SLOTS, len(pieces[0]) * P]
             queries = [step_view(rows[GATE], step, blocks) for blocks in pieces]
             backs = []
             for blocks in pieces:
                 pool = psum_in if last and blocks[0] == 0 else psum_back
                 c_back = tokens_onto_partitions(CANDIDATE, c_values[step], blocks, pool)
-                if u_back is None or blocks[0]:
-                    u_back = tokens_onto_partitions(GATE, u_values[step], blocks, pool)
-                backs.append((u_back, c_back))
+                backs.append((tokens_onto_partitions(GATE, u_values[step], blocks, pool), c_back))
             differences, products = [], []
             for (u_back, c_back), query in zip(backs, queries):
                 difference = blend.tile(shape, F32, name="difference")
                 nc.vector.tensor_tensor(out=difference[:], in0=c_back[:], in1=query, op=ALU.subtract)
                 differences.append(difference)
-            if key is not None:
-                sorted_words[key] = split_words(*key)
             for (u_back, c_back), difference in zip(backs, differences):
                 product = blend.tile(shape, F32, name="product")
                 nc.vector.tensor_tensor(out=product[:], in0=u_back[:], in1=difference[:], op=ALU.mult)
@@ -250,11 +246,11 @@ def tile_gatedcrossattention_pb_kernel(
         load_weights(GATE, 1)
         load_weight_scales(CANDIDATE)
         load_weights(CANDIDATE, 0)
-        load_weights(CANDIDATE, 1)
         load_rows(GATE, 1)
+        load_weights(CANDIDATE, 1)
+        load_rows(CANDIDATE, 1)
         load_weights(GATE, 2)
         load_weights(CANDIDATE, 2)
-        load_rows(CANDIDATE, 1)
         load_weights(GATE, 3)
         load_weights(CANDIDATE, 3)
         for quarter in range(2, QUARTERS):
@@ -289,29 +285,27 @@ def tile_gatedcrossattention_pb_kernel(
         u_values[1] = project(GATE, 1, psum_in.tile([P, 2, QUARTER_TOKENS], F32, name="flipped"))
         bias_onto_partitions(CANDIDATE)
         c_values[0] = project(CANDIDATE, 0)
-        c_values[1] = project(CANDIDATE, 1, psum_back.tile([P, 2, QUARTER_TOKENS], F32, name="back_" + PATH_NAMES[GATE]))
 
         later_paths = [(path, quarter) for quarter in range(1, QUARTERS) for path in PATHS]
         later_inputs = [(path, quarter, group) for path, quarter in later_paths for group in range(K_GROUPS)]
         sorted_words = {}
         waiting = []
-        for r in range(1, STEPS):
-            if r >= 2:
+        for r in range(STEPS):
+            if r not in u_values:
                 u_values[r] = project(GATE, r)
-                if r < STEPS - 1:
-                    c_values[r] = project(CANDIDATE, r)
+            if r not in c_values and r < STEPS - 1:
+                c_values[r] = project(CANDIDATE, r)
+            if r == 1:
+                sorted_words[later_paths[1]] = split_words(*later_paths[1])
             for job in waiting:
                 quantise(*job)
-            if r % 2 == 0 and r // 2 + 1 < len(later_paths):
+            if r >= 2 and r % 2 == 0 and r // 2 + 1 < len(later_paths):
                 sorted_words[later_paths[r // 2 + 1]] = split_words(*later_paths[r // 2 + 1])
-            jobs = later_inputs[0:2] if r == 1 else later_inputs[2:4] if r == 2 else later_inputs[r + 1 : r + 2]
-            early = r == 1
-            if early:
-                early_u = tokens_onto_partitions(GATE, u_values[0], [0, 1], psum_back)
-                waiting = [features_onto_partitions(*job, nc.scalar.copy, sorted_words.get(job[:2])) for job in jobs]
-            key = later_paths[1] if r == 1 else None
-            blend_and_store(r - 1, [[0, 1]], nc.gpsimd, key=key, u_back=early_u if r == 1 else None)
-            if not early:
-                waiting = [features_onto_partitions(*job, nc.scalar.copy, sorted_words.get(job[:2])) for job in jobs]
+            if r >= 1:
+                blend_and_store(r - 1, [[0, 1]], nc.gpsimd)
+            waiting = [
+                features_onto_partitions(*job, nc.scalar.copy, sorted_words.get(job[:2]))
+                for job in (later_inputs[:2] if r == 0 else later_inputs[r + 1 : r + 2])
+            ]
         c_values[STEPS - 1] = project(CANDIDATE, STEPS - 1)
         blend_and_store(STEPS - 1, [[0], [1]], nc.vector, last=True)

@@ -78,11 +78,12 @@ def tile_gatedcrossattention_pb_kernel(
         x_codes = keep.tile([P, 2, QUARTERS, K_GROUPS, QUARTER_TOKENS], U32, align_bytes=64)
         x_planes = keep.tile([P, 2, QUARTERS, K_GROUPS, QUARTER_TOKENS], U8, align_bytes=64)
         identity = keep.tile([P, P], F32)
-        bias_rows = [keep.tile([P, P], BF16, name="bias_rows_" + PATH_NAMES[path]) for path in PATHS]
-        bias_rows_f32 = [keep.tile([P, P], F32, name="bias_f32_" + PATH_NAMES[path]) for path in PATHS]
-        bias_cols = [keep.tile([P, BLOCKS], F32, name="bias_cols_" + PATH_NAMES[path]) for path in PATHS]
+        bias_rows = keep.tile([P, P], BF16)
+        bias_rows_f32 = keep.tile([P, P], F32)
+        bias_cols = keep.tile([P, 2 * BLOCKS], F32)
         table_warmer = keep.tile([P, 1], F32)
         zeros = keep.tile([P, 2 * P], BF16)
+        port_order = keep.tile([P, 1], F32)
 
         def load_rows(path, quarter):
             slots = slice(quarter * QUARTER_SLOTS, (quarter + 1) * QUARTER_SLOTS)
@@ -160,14 +161,14 @@ def tile_gatedcrossattention_pb_kernel(
 
         def activate(path, step, acc):
             value = turned.tile([P, STEP_BLOCKS, QUARTER_TOKENS], F32, name="turned_" + PATH_NAMES[path])
-            first_column = step % QUARTER_STEPS * STEP_BLOCKS
+            first_column = path * BLOCKS + step % QUARTER_STEPS * STEP_BLOCKS
             for j in range(STEP_BLOCKS):
                 column = first_column + j
                 nc.scalar.activation(
                     out=value[:, j, :],
                     in_=acc[:, j, :],
                     func=FUNCTIONS[path],
-                    bias=bias_cols[path][:, column : column + 1],
+                    bias=bias_cols[:, column : column + 1],
                     scale=1.0,
                 )
             return value
@@ -204,11 +205,13 @@ def tile_gatedcrossattention_pb_kernel(
             differences, products = [], []
             for (u_back, c_back), query in zip(backs, queries):
                 difference = blend.tile(shape, F32, name="difference")
-                nc.vector.tensor_tensor(out=difference[:], in0=c_back[:], in1=query, op=ALU.subtract)
+                for s in range(QUARTER_SLOTS):
+                    nc.vector.tensor_tensor(out=difference[:, s, :], in0=c_back[:, s, :], in1=query[:, s, :], op=ALU.subtract)
                 differences.append(difference)
             for (u_back, c_back), difference in zip(backs, differences):
                 product = blend.tile(shape, F32, name="product")
-                nc.vector.tensor_tensor(out=product[:], in0=u_back[:], in1=difference[:], op=ALU.mult)
+                for s in range(QUARTER_SLOTS):
+                    nc.vector.tensor_tensor(out=product[:, s, :], in0=u_back[:, s, :], in1=difference[:, s, :], op=ALU.mult)
                 products.append(product)
             for blocks, query, product in zip(pieces, queries, products):
                 result = results.tile(shape, F32, name="result")
@@ -221,28 +224,28 @@ def tile_gatedcrossattention_pb_kernel(
                 nc.tensor.matmul(unread[:, 0, :], zeros[:, 0:P], zeros[:], start=True, stop=True)
 
         def load_bias(path):
-            nc.scalar.dma_start(out=bias_rows[path][0:BLOCKS, :], in_=bias_dram[path])
+            nc.scalar.dma_start(out=bias_rows[path * BLOCKS : (path + 1) * BLOCKS, :], in_=bias_dram[path])
 
-        def bias_onto_partitions(path):
+        def bias_onto_partitions():
             flipped = psum_back.tile([P, 2, QUARTER_TOKENS], F32, name="back_" + PATH_NAMES[GATE])
-            nc.tensor.transpose(flipped[:, 0, 0:P], bias_rows_f32[path][:], identity[:])
-            nc.vector.tensor_copy(out=bias_cols[path][:], in_=flipped[:, 0, 0:BLOCKS])
+            nc.tensor.transpose(flipped[:, 0, 0:P], bias_rows_f32[:], identity[:])
+            nc.vector.tensor_copy(out=bias_cols[:], in_=flipped[:, 0, 0 : 2 * BLOCKS])
 
-        nc.vector.memset(bias_rows[GATE][:], 0.0)
+        nc.vector.memset(bias_rows[:], 0.0)
         nc.vector.memset(w_planes[GATE][:].bitcast(I32), 0)
-        nc.vector.memset(table_warmer[:], 0.0)
-        nc.vector.memset(zeros[:], 0.0)
-        nc.vector.memset(bias_rows[CANDIDATE][:], 0.0)
         nc.vector.memset(w_planes[CANDIDATE][:].bitcast(I32), 0)
+        nc.vector.memset(zeros[:], 0.0)
+        nc.vector.memset(table_warmer[:], 0.0)
+        for path in PATHS:
+            load_bias(path)
         nc.scalar.activation(out=table_warmer[:], in_=table_warmer[:], func=ACT.Sigmoid)
+        nc.gpsimd.tensor_copy(out=port_order[:], in_=zeros[:, 0:2].bitcast(F32))
         make_identity(nc, identity[:])
 
         load_rows(GATE, 0)
         load_weight_scales(GATE)
         load_weights(GATE, 0)
         load_rows(CANDIDATE, 0)
-        load_bias(GATE)
-        load_bias(CANDIDATE)
         load_weights(GATE, 1)
         load_weight_scales(CANDIDATE)
         load_weights(CANDIDATE, 0)
@@ -270,20 +273,18 @@ def tile_gatedcrossattention_pb_kernel(
             ]
 
         u_values, c_values = {}, {}
-        for path in PATHS:
-            nc.gpsimd.tensor_copy(out=bias_rows_f32[path][:], in_=bias_rows[path][:])
-        keep_clock_up(9)
+        nc.gpsimd.tensor_copy(out=bias_rows_f32[:], in_=bias_rows[:])
+        keep_clock_up(18)
         first = first_quarter(GATE)
         keep_clock_up(4)
         for job in first:
             quantise(*job)
         first = first_quarter(CANDIDATE)
-        bias_onto_partitions(GATE)
+        bias_onto_partitions()
         u_values[0] = project(GATE, 0)
         for job in first:
             quantise(*job)
         u_values[1] = project(GATE, 1, psum_in.tile([P, 2, QUARTER_TOKENS], F32, name="flipped"))
-        bias_onto_partitions(CANDIDATE)
         c_values[0] = project(CANDIDATE, 0)
 
         later_paths = [(path, quarter) for quarter in range(1, QUARTERS) for path in PATHS]

@@ -68,15 +68,23 @@ def tile_gatedcrossattention_pb_kernel(
             for path in PATHS
         ]
         w_codes = [
-            keep.tile([P, K_GROUPS, FEATURES], U32, align_bytes=64, name="w_codes_" + PATH_NAMES[path])
+            keep.tile([P, K_GROUPS, FEATURES], U32, align_bytes=256, name="w_codes_" + PATH_NAMES[path])
             for path in PATHS
         ]
-        w_planes = [
-            keep.tile([P, FEATURES], U8, align_bytes=64, name="w_planes_" + PATH_NAMES[path])
+        pad_bytes = 64
+        w_planes_padded = [
+            keep.tile([P, pad_bytes + FEATURES], U8, align_bytes=256, name="w_planes_" + PATH_NAMES[path])
             for path in PATHS
         ]
-        x_codes = keep.tile([P, 2, QUARTERS, K_GROUPS, QUARTER_TOKENS], U32, align_bytes=64)
-        x_planes = keep.tile([P, 2, QUARTERS, K_GROUPS, QUARTER_TOKENS], U8, align_bytes=64)
+        w_planes = [tile[:, pad_bytes:] for tile in w_planes_padded]
+        x_codes_padded = keep.tile([P, 2 * pad_bytes // 4 + 2 * QUARTERS * K_GROUPS * QUARTER_TOKENS], U32, align_bytes=256)
+        x_codes = x_codes_padded[:, 2 * pad_bytes // 4 :].rearrange(
+            "p (a q g n) -> p a q g n", a=2, q=QUARTERS, g=K_GROUPS
+        )
+        x_planes_padded = keep.tile([P, 3 * pad_bytes + 2 * QUARTERS * K_GROUPS * QUARTER_TOKENS], U8, align_bytes=256)
+        x_planes = x_planes_padded[:, 3 * pad_bytes :].rearrange(
+            "p (a q g n) -> p a q g n", a=2, q=QUARTERS, g=K_GROUPS
+        )
         identity = keep.tile([P, P], F32)
         bias_rows = keep.tile([P, P], BF16)
         bias_rows_f32 = keep.tile([P, P], F32)
@@ -232,8 +240,8 @@ def tile_gatedcrossattention_pb_kernel(
             nc.vector.tensor_copy(out=bias_cols[:], in_=flipped[:, 0, 0 : 2 * BLOCKS])
 
         nc.vector.memset(bias_rows[:], 0.0)
-        nc.vector.memset(w_planes[GATE][:].bitcast(I32), 0)
-        nc.vector.memset(w_planes[CANDIDATE][:].bitcast(I32), 0)
+        nc.vector.memset(w_planes_padded[GATE][:].bitcast(I32), 0)
+        nc.vector.memset(w_planes_padded[CANDIDATE][:].bitcast(I32), 0)
         nc.vector.memset(zeros[:], 0.0)
         nc.vector.memset(table_warmer[:], 0.0)
         for path in PATHS:

@@ -57,7 +57,7 @@ def tile_gatedcrossattention_pb_kernel(
         turned = ctx.enter_context(tc.tile_pool(name="turned", bufs=4))
         blend = ctx.enter_context(tc.tile_pool(name="blend", bufs=3))
         split = ctx.enter_context(tc.tile_pool(name="split", bufs=3))
-        results = ctx.enter_context(tc.tile_pool(name="results", bufs=4))
+        results = ctx.enter_context(tc.tile_pool(name="results", bufs=6))
         psum_in = ctx.enter_context(tc.psum_pool(name="psum_in", bufs=2))
         psum_mx = ctx.enter_context(tc.psum_pool(name="psum_mx", bufs=1))
         psum_back = ctx.enter_context(tc.psum_pool(name="psum_back", bufs=2))
@@ -223,8 +223,9 @@ def tile_gatedcrossattention_pb_kernel(
                 products.append(product)
             for blocks, query, product in zip(pieces, queries, products):
                 result = results.tile(shape, F32, name="result")
-                adder.tensor_tensor(out=result[:], in0=product[:], in1=query, op=ALU.add)
-                nc.sync.dma_start(out=step_view(out_dram, step, blocks), in_=result[:])
+                for slots in ([slice(0, 1), slice(1, 2)] if step >= STEPS - 2 else [slice(0, 2)]):
+                    adder.tensor_tensor(out=result[:, slots, :], in0=product[:, slots, :], in1=query[:, slots, :], op=ALU.add)
+                    nc.sync.dma_start(out=step_view(out_dram, step, blocks)[:, slots, :], in_=result[:, slots, :])
 
         def keep_clock_up(passes):
             unread = psum_back.tile([P, 2, QUARTER_TOKENS], F32, name="back_" + PATH_NAMES[GATE])
@@ -239,8 +240,8 @@ def tile_gatedcrossattention_pb_kernel(
             nc.tensor.transpose(flipped[:, 0, 0:P], bias_rows_f32[:], identity[:])
             nc.vector.tensor_copy(out=bias_cols[:], in_=flipped[:, 0, 0 : 2 * BLOCKS])
 
-        nc.vector.memset(bias_rows[:], 0.0)
         nc.vector.memset(w_planes_padded[GATE][:].bitcast(I32), 0)
+        nc.vector.memset(bias_rows[:], 0.0)
         nc.vector.memset(w_planes_padded[CANDIDATE][:].bitcast(I32), 0)
         nc.vector.memset(zeros[:], 0.0)
         nc.vector.memset(table_warmer[:], 0.0)
@@ -250,12 +251,12 @@ def tile_gatedcrossattention_pb_kernel(
         nc.gpsimd.tensor_copy(out=port_order[:], in_=zeros[:, 0:2].bitcast(F32))
         make_identity(nc, identity[:])
 
-        load_rows(GATE, 0)
         load_weight_scales(GATE)
-        load_weights(GATE, 0)
+        load_rows(GATE, 0)
         load_rows(CANDIDATE, 0)
-        load_weights(GATE, 1)
+        load_weights(GATE, 0)
         load_weight_scales(CANDIDATE)
+        load_weights(GATE, 1)
         load_weights(CANDIDATE, 0)
         load_rows(GATE, 1)
         load_weights(CANDIDATE, 1)
@@ -282,7 +283,7 @@ def tile_gatedcrossattention_pb_kernel(
 
         u_values, c_values = {}, {}
         nc.gpsimd.tensor_copy(out=bias_rows_f32[:], in_=bias_rows[:])
-        keep_clock_up(18)
+        keep_clock_up(24)
         first = first_quarter(GATE)
         keep_clock_up(4)
         for job in first:

@@ -283,7 +283,7 @@ def tile_gatedcrossattention_pb_kernel(
 
         u_values, c_values = {}, {}
         nc.gpsimd.tensor_copy(out=bias_rows_f32[:], in_=bias_rows[:])
-        keep_clock_up(24)
+        keep_clock_up(13)
         first = first_quarter(GATE)
         keep_clock_up(4)
         for job in first:

@@ -240,8 +240,8 @@ def tile_gatedcrossattention_pb_kernel(
             nc.tensor.transpose(flipped[:, 0, 0:P], bias_rows_f32[:], identity[:])
             nc.vector.tensor_copy(out=bias_cols[:], in_=flipped[:, 0, 0 : 2 * BLOCKS])
 
-        nc.vector.memset(w_planes_padded[GATE][:].bitcast(I32), 0)
         nc.vector.memset(bias_rows[:], 0.0)
+        nc.vector.memset(w_planes_padded[GATE][:].bitcast(I32), 0)
         nc.vector.memset(w_planes_padded[CANDIDATE][:].bitcast(I32), 0)
         nc.vector.memset(zeros[:], 0.0)
         nc.vector.memset(table_warmer[:], 0.0)
@@ -251,8 +251,8 @@ def tile_gatedcrossattention_pb_kernel(
         nc.gpsimd.tensor_copy(out=port_order[:], in_=zeros[:, 0:2].bitcast(F32))
         make_identity(nc, identity[:])
 
-        load_weight_scales(GATE)
         load_rows(GATE, 0)
+        load_weight_scales(GATE)
         load_rows(CANDIDATE, 0)
         load_weights(GATE, 0)
         load_weight_scales(CANDIDATE)
@@ -283,7 +283,7 @@ def tile_gatedcrossattention_pb_kernel(
 
         u_values, c_values = {}, {}
         nc.gpsimd.tensor_copy(out=bias_rows_f32[:], in_=bias_rows[:])
-        keep_clock_up(13)
+        keep_clock_up(10)
         first = first_quarter(GATE)
         keep_clock_up(4)
         for job in first:

from contextlib import ExitStack

import concourse.mybir as mybir
from concourse.masks import make_identity

F32 = mybir.dt.float32
BF16 = mybir.dt.bfloat16
I32 = mybir.dt.int32
U32 = mybir.dt.uint32
U8 = mybir.dt.uint8
FP8X4 = mybir.dt.float8_e4m3fn_x4
ACT = mybir.ActivationFunctionType
ALU = mybir.AluOpType

P = 128
TOKENS = 1024
FEATURES = 1024
K_PASS = 4 * P
K_GROUPS = FEATURES // K_PASS
WORDS = K_PASS // 2
SLOTS = TOKENS // P
QUARTER_SLOTS = 2
QUARTERS = SLOTS // QUARTER_SLOTS
QUARTER_TOKENS = QUARTER_SLOTS * P
BLOCKS = FEATURES // P
STEP_BLOCKS = 2
STEP_FEATURES = STEP_BLOCKS * P
QUARTER_STEPS = BLOCKS // STEP_BLOCKS
STEPS = QUARTERS * QUARTER_STEPS

GATE, CANDIDATE = 0, 1
PATHS = (GATE, CANDIDATE)
PATH_NAMES = ("gate", "candidate")
FUNCTIONS = (ACT.Sigmoid, ACT.Tanh)

FLOPS = 2 * 2 * TOKENS * FEATURES * FEATURES


def tile_gatedcrossattention_pb_kernel(
    tc, query, hr, Wu_words, Wu_scales, bu, Wh_words, Wh_scales, bh, out
):
    nc = tc.nc

    rows_dram = [
        x.flatten_outer_dims().rearrange("(p s) e -> p s e", s=SLOTS) for x in (query, hr)
    ]
    out_dram = out.flatten_outer_dims().rearrange("(p s) e -> p s e", s=SLOTS)
    w_codes_dram = [
        w.rearrange("g p n t -> p g (n t)").bitcast(I32) for w in (Wu_words, Wh_words)
    ]
    w_scales_dram = [Wu_scales, Wh_scales]
    bias_dram = [b.rearrange("(b n) -> b n", n=P) for b in (bu, bh)]

    with ExitStack() as ctx:
        keep = ctx.enter_context(tc.tile_pool(name="keep", bufs=1))
        stage = ctx.enter_context(tc.tile_pool(name="stage", bufs=4))
        turned = ctx.enter_context(tc.tile_pool(name="turned", bufs=4))
        blend = ctx.enter_context(tc.tile_pool(name="blend", bufs=3))
        split = ctx.enter_context(tc.tile_pool(name="split", bufs=3))
        results = ctx.enter_context(tc.tile_pool(name="results", bufs=6))
        psum_in = ctx.enter_context(tc.psum_pool(name="psum_in", bufs=2))
        psum_mx = ctx.enter_context(tc.psum_pool(name="psum_mx", bufs=1))
        psum_back = ctx.enter_context(tc.psum_pool(name="psum_back", bufs=2))
        ctx.enter_context(tc.manual_schedule())

        rows = [
            keep.tile([P, SLOTS, FEATURES], BF16, name="rows_" + PATH_NAMES[path])
            for path in PATHS
        ]
        w_codes = [
            keep.tile([P, K_GROUPS, FEATURES], U32, align_bytes=256, name="w_codes_" + PATH_NAMES[path])
            for path in PATHS
        ]
        pad_bytes = 64
        w_planes_padded = [
            keep.tile([P, pad_bytes + FEATURES], U8, align_bytes=256, name="w_planes_" + PATH_NAMES[path])
            for path in PATHS
        ]
        w_planes = [tile[:, pad_bytes:] for tile in w_planes_padded]
        x_codes_padded = keep.tile([P, 2 * pad_bytes // 4 + 2 * QUARTERS * K_GROUPS * QUARTER_TOKENS], U32, align_bytes=256)
        x_codes = x_codes_padded[:, 2 * pad_bytes // 4 :].rearrange(
            "p (a q g n) -> p a q g n", a=2, q=QUARTERS, g=K_GROUPS
        )
        x_planes_padded = keep.tile([P, 3 * pad_bytes + 2 * QUARTERS * K_GROUPS * QUARTER_TOKENS], U8, align_bytes=256)
        x_planes = x_planes_padded[:, 3 * pad_bytes :].rearrange(
            "p (a q g n) -> p a q g n", a=2, q=QUARTERS, g=K_GROUPS
        )
        identity = keep.tile([P, P], F32)
        bias_rows = keep.tile([P, P], BF16)
        bias_rows_f32 = keep.tile([P, P], F32)
        bias_cols = keep.tile([P, 2 * BLOCKS], F32)
        table_warmer = keep.tile([P, 1], F32)
        zeros = keep.tile([P, 2 * P], BF16)
        port_order = keep.tile([P, 1], F32)

        def load_rows(path, quarter):
            slots = slice(quarter * QUARTER_SLOTS, (quarter + 1) * QUARTER_SLOTS)
            nc.sync.dma_start(out=rows[path][:, slots, :], in_=rows_dram[path][:, slots, :])

        def load_weight_scales(path):
            for quadrant in range(4):
                first = 32 * quadrant
                nc.sync.dma_start(
                    out=w_planes[path][first : first + 4 * K_GROUPS, :].bitcast(I32),
                    in_=w_scales_dram[path][:, 4 * quadrant : 4 * quadrant + 4, :].bitcast(I32),
                )

        def load_weights(path, pair):
            cols = slice(pair * STEP_FEATURES, (pair + 1) * STEP_FEATURES)
            nc.sync.dma_start(
                out=w_codes[path][:, :, cols].bitcast(I32), in_=w_codes_dram[path][:, :, cols]
            )

        def split_words(path, quarter):
            slots = slice(quarter * QUARTER_SLOTS, (quarter + 1) * QUARTER_SLOTS)
            sorted_words = split.tile([P, QUARTER_SLOTS, K_GROUPS, 2, P], F32, name="sorted_words")
            nc.vector.tensor_copy(
                out=sorted_words[:],
                in_=rows[path][:, slots, :]
                .rearrange("p s e -> p (s e)")
                .bitcast(F32)
                .rearrange("p (s g w h) -> p s g h w", s=QUARTER_SLOTS, g=K_GROUPS, h=2),
            )
            return sorted_words

        def features_onto_partitions(path, quarter, group, copy, sorted_words=None, flipped=None):
            if flipped is None:
                flipped = psum_in.tile([P, 2, QUARTER_TOKENS], F32, name="flipped")
            for h in range(2):
                for j in range(QUARTER_SLOTS):
                    if sorted_words is None:
                        words = rows[path][:, quarter * QUARTER_SLOTS + j, :].bitcast(F32)
                        words = words[:, group * WORDS + h : (group + 1) * WORDS : 2]
                    else:
                        words = sorted_words[:, j, group, h, :]
                    nc.tensor.transpose(flipped[:, h, j * P : (j + 1) * P], words, identity[:])
            grouped = stage.tile([P, 4 * QUARTER_TOKENS], BF16, align_bytes=64, name="grouped")
            copy(
                out=grouped[:].bitcast(F32).rearrange("p (c h) -> p c h", h=2),
                in_=flipped[:].rearrange("p h c -> p c h"),
            )
            return (path, quarter, group, grouped)

        def quantise(path, quarter, group, grouped):
            nc.vector.quantize_mx(
                out=x_codes[:, path, quarter, group, :].bitcast(FP8X4),
                scales=x_planes[:, path, quarter, group, :],
                in_=grouped[:],
            )

        def multiply(path, step, acc=None):
            quarter, pair = divmod(step, QUARTER_STEPS)
            if acc is None:
                acc = psum_mx.tile([P, STEP_BLOCKS, QUARTER_TOKENS], F32, name="acc_" + PATH_NAMES[path])
            for j in range(STEP_BLOCKS):
                block = pair * STEP_BLOCKS + j
                cols = slice(block * P, (block + 1) * P)
                for group in range(K_GROUPS):
                    nc.tensor.matmul_mx(
                        out=acc[:, j, :],
                        lhsT=w_codes[path][:, group, cols].bitcast(FP8X4),
                        lhsT_scale=w_planes[path][4 * group : P, cols],
                        rhs=x_codes[:, path, quarter, group, :].bitcast(FP8X4),
                        rhs_scale=x_planes[:, path, quarter, group, :],
                        start=(group == 0),
                        stop=(group == K_GROUPS - 1),
                    )
            return acc

        def activate(path, step, acc):
            value = turned.tile([P, STEP_BLOCKS, QUARTER_TOKENS], F32, name="turned_" + PATH_NAMES[path])
            first_column = path * BLOCKS + step % QUARTER_STEPS * STEP_BLOCKS
            for j in range(STEP_BLOCKS):
                column = first_column + j
                nc.scalar.activation(
                    out=value[:, j, :],
                    in_=acc[:, j, :],
                    func=FUNCTIONS[path],
                    bias=bias_cols[:, column : column + 1],
                    scale=1.0,
                )
            return value

        def project(path, step, acc=None):
            return activate(path, step, multiply(path, step, acc))

        def tokens_onto_partitions(path, value, blocks, pool):
            back = pool.tile([P, QUARTER_SLOTS, len(blocks) * P], F32, name="flipped" if pool is psum_in else "back_" + PATH_NAMES[path])
            for s in range(QUARTER_SLOTS):
                for i, j in enumerate(blocks):
                    nc.tensor.transpose(
                        back[:, s, i * P : (i + 1) * P], value[:, j, s * P : (s + 1) * P], identity[:]
                    )
            return back

        def step_view(tensor, step, blocks):
            quarter, pair = divmod(step, QUARTER_STEPS)
            first = pair * STEP_FEATURES + blocks[0] * P
            return tensor[
                :,
                quarter * QUARTER_SLOTS : (quarter + 1) * QUARTER_SLOTS,
                first : first + len(blocks) * P,
            ]

        def blend_and_store(step, pieces, adder, last=False):
            shape = [P, QUARTER_SLOTS, len(pieces[0]) * P]
            queries = [step_view(rows[GATE], step, blocks) for blocks in pieces]
            backs = []
            for blocks in pieces:
                pool = psum_in if last and blocks[0] == 0 else psum_back
                c_back = tokens_onto_partitions(CANDIDATE, c_values[step], blocks, pool)
                backs.append((tokens_onto_partitions(GATE, u_values[step], blocks, pool), c_back))
            differences, products = [], []
            for (u_back, c_back), query in zip(backs, queries):
                difference = blend.tile(shape, F32, name="difference")
                for s in range(QUARTER_SLOTS):
                    nc.vector.tensor_tensor(out=difference[:, s, :], in0=c_back[:, s, :], in1=query[:, s, :], op=ALU.subtract)
                differences.append(difference)
            for (u_back, c_back), difference in zip(backs, differences):
                product = blend.tile(shape, F32, name="product")
                for s in range(QUARTER_SLOTS):
                    nc.vector.tensor_tensor(out=product[:, s, :], in0=u_back[:, s, :], in1=difference[:, s, :], op=ALU.mult)
                products.append(product)
            for blocks, query, product in zip(pieces, queries, products):
                result = results.tile(shape, F32, name="result")
                for slots in ([slice(0, 1), slice(1, 2)] if step >= STEPS - 2 else [slice(0, 2)]):
                    adder.tensor_tensor(out=result[:, slots, :], in0=product[:, slots, :], in1=query[:, slots, :], op=ALU.add)
                    nc.sync.dma_start(out=step_view(out_dram, step, blocks)[:, slots, :], in_=result[:, slots, :])

        def keep_clock_up(passes):
            unread = psum_back.tile([P, 2, QUARTER_TOKENS], F32, name="back_" + PATH_NAMES[GATE])
            for i in range(passes):
                nc.tensor.matmul(unread[:, 0, :], zeros[:, 0:P], zeros[:], start=True, stop=True)

        def load_bias(path):
            nc.scalar.dma_start(out=bias_rows[path * BLOCKS : (path + 1) * BLOCKS, :], in_=bias_dram[path])

        def bias_onto_partitions():
            flipped = psum_back.tile([P, 2, QUARTER_TOKENS], F32, name="back_" + PATH_NAMES[GATE])
            nc.tensor.transpose(flipped[:, 0, 0:P], bias_rows_f32[:], identity[:])
            nc.vector.tensor_copy(out=bias_cols[:], in_=flipped[:, 0, 0 : 2 * BLOCKS])

        nc.vector.memset(bias_rows[:], 0.0)
        nc.vector.memset(w_planes_padded[GATE][:].bitcast(I32), 0)
        nc.vector.memset(w_planes_padded[CANDIDATE][:].bitcast(I32), 0)
        nc.vector.memset(zeros[:], 0.0)
        nc.vector.memset(table_warmer[:], 0.0)
        for path in PATHS:
            load_bias(path)
        nc.scalar.activation(out=table_warmer[:], in_=table_warmer[:], func=ACT.Sigmoid)
        nc.gpsimd.tensor_copy(out=port_order[:], in_=zeros[:, 0:2].bitcast(F32))
        make_identity(nc, identity[:])

        load_rows(GATE, 0)
        load_weight_scales(GATE)
        load_rows(CANDIDATE, 0)
        load_weights(GATE, 0)
        load_weight_scales(CANDIDATE)
        load_weights(GATE, 1)
        load_weights(CANDIDATE, 0)
        load_rows(GATE, 1)
        load_weights(CANDIDATE, 1)
        load_rows(CANDIDATE, 1)
        load_weights(GATE, 2)
        load_weights(CANDIDATE, 2)
        load_weights(GATE, 3)
        load_weights(CANDIDATE, 3)
        for quarter in range(2, QUARTERS):
            for path in PATHS:
                load_rows(path, quarter)

        def first_quarter(path):
            banks = [None, None]
            if path == CANDIDATE:
                banks = [
                    psum_back.tile([P, 2, QUARTER_TOKENS], F32, name="back_" + PATH_NAMES[CANDIDATE])
                    for group in range(K_GROUPS)
                ]
            return [
                features_onto_partitions(path, 0, 0, nc.vector.tensor_copy, None, banks[0]),
                features_onto_partitions(path, 0, 1, nc.scalar.copy, None, banks[1]),
            ]

        u_values, c_values = {}, {}
        nc.gpsimd.tensor_copy(out=bias_rows_f32[:], in_=bias_rows[:])
        keep_clock_up(10)
        first = first_quarter(GATE)
        keep_clock_up(4)
        for job in first:
            quantise(*job)
        first = first_quarter(CANDIDATE)
        bias_onto_partitions()
        u_values[0] = project(GATE, 0)
        for job in first:
            quantise(*job)
        u_values[1] = project(GATE, 1, psum_in.tile([P, 2, QUARTER_TOKENS], F32, name="flipped"))
        c_values[0] = project(CANDIDATE, 0)

        later_paths = [(path, quarter) for quarter in range(1, QUARTERS) for path in PATHS]
        later_inputs = [(path, quarter, group) for path, quarter in later_paths for group in range(K_GROUPS)]
        sorted_words = {}
        waiting = []
        for r in range(STEPS):
            if r not in u_values:
                u_values[r] = project(GATE, r)
            if r not in c_values and r < STEPS - 1:
                c_values[r] = project(CANDIDATE, r)
            if r == 1:
                sorted_words[later_paths[1]] = split_words(*later_paths[1])
            for job in waiting:
                quantise(*job)
            if r >= 2 and r % 2 == 0 and r // 2 + 1 < len(later_paths):
                sorted_words[later_paths[r // 2 + 1]] = split_words(*later_paths[r // 2 + 1])
            if r >= 1:
                blend_and_store(r - 1, [[0, 1]], nc.gpsimd)
            waiting = [
                features_onto_partitions(*job, nc.scalar.copy, sorted_words.get(job[:2]))
                for job in (later_inputs[:2] if r == 0 else later_inputs[r + 1 : r + 2])
            ]
        c_values[STEPS - 1] = project(CANDIDATE, STEPS - 1)
        blend_and_store(STEPS - 1, [[0], [1]], nc.vector, last=True)
